import numpy as np
import ml_dtypes


def mxq(x, axis, fmt="e4m3"):
    dtype, down = {"e4m3": (ml_dtypes.float8_e4m3fn, 7), "e5m2": (ml_dtypes.float8_e5m2, 14)}[fmt]
    v = np.moveaxis(np.asarray(x, np.float32).astype(ml_dtypes.bfloat16).astype(np.float64), axis, -1)
    blocks = v.reshape(v.shape[:-1] + (-1, 32))
    amax = np.abs(blocks).max(-1, keepdims=True)
    byte = np.maximum(np.where(amax > 0, np.frexp(amax)[1] - 1 + 127, 0) - down, 1)
    scale = np.exp2(byte - 127.0)
    codes = (blocks / scale).astype(np.float32).astype(dtype).astype(np.float64)
    return np.moveaxis((codes * scale).reshape(v.shape), -1, axis)


WIDE = False


def mx_kscale(k):
    if not WIDE:
        return np.ones(k)
    levels = np.array([10, -10, 5, -5, 0])
    a = np.random.permutation(np.resize(levels, k // 512 * 4)).reshape(k // 512, 4)
    idx = np.arange(k)
    return np.exp2(a[idx // 512, idx % 128 // 32])


BF16 = ml_dtypes.bfloat16


def bf(x):
    return np.asarray(x, np.float32).astype(BF16)


def f64(x):
    return np.asarray(x).astype(np.float64)


E2M1 = np.array([0.0, 0.5, 1.0, 1.5, 2.0, 3.0, 4.0, 6.0, -0.0, -0.5, -1.0, -1.5, -2.0, -3.0, -4.0, -6.0])


def pack_weight(w, fmt):
    k, n = w.shape
    w = f64(bf(w)).reshape(k // 32, 32, n)
    amax = np.abs(w).max(1)
    if fmt == "e4m3":
        byte = np.frexp(amax)[1] - 1 + 127 - 7
    else:
        mant, ex = np.frexp(amax / 6.0)
        byte = np.where(mant > 0.5, ex, ex - 1) + 127
    byte = np.clip(np.where(amax > 0, byte, 1), 1, 254)
    scaled = (w * np.exp2(127.0 - byte)[:, None, :]).reshape(k, n).astype(np.float32)
    by_word = np.ascontiguousarray(scaled.reshape(k // 512, 128, 4, n).transpose(0, 1, 3, 2))
    if fmt == "e4m3":
        words = by_word.astype(ml_dtypes.float8_e4m3fn).view(np.uint8)
    else:
        c = by_word.astype(ml_dtypes.float4_e2m1fn).view(np.uint8) & 0xF
        words = c[..., 0::2] | (c[..., 1::2] << 4)
    return np.ascontiguousarray(words), np.ascontiguousarray(byte.astype(np.uint8).reshape(k // 512, 16, n))


def unpack_weight(words, scales, fmt):
    g, p, n, _ = words.shape
    if fmt == "e4m3":
        vals = np.ascontiguousarray(words).view(ml_dtypes.float8_e4m3fn).astype(np.float64)
    else:
        nib = np.empty((g, p, n, 4), np.uint8)
        nib[..., 0::2] = words & 0xF
        nib[..., 1::2] = words >> 4
        vals = E2M1[nib]
    vals = vals * np.repeat(np.exp2(scales.astype(np.float64) - 127.0), 8, axis=1)[..., None]
    return vals.transpose(0, 1, 3, 2).reshape(g * 512, n)


B, S, HIDDEN, NUM_HEADS, HEAD_DIM = 1, 128, 3072, 16, 128
F = NUM_HEADS * HEAD_DIM
FMT = "e4m3"


def _split_heads(x):
    b, s, _ = x.shape
    return x.reshape(b, s, NUM_HEADS, HEAD_DIM).transpose(0, 2, 1, 3)


def setup_inputs():
    s = mx_kscale(HIDDEN)
    scale = 1.0 / np.sqrt(HIDDEN)
    hidden_states = bf(np.random.standard_normal((B, S, HIDDEN)) * s)
    Wq_words, Wq_scales = pack_weight(np.random.standard_normal((HIDDEN, F)) * scale / s[:, None], FMT)
    bq = bf(np.random.standard_normal(F) * 0.5)
    Wk_words, Wk_scales = pack_weight(np.random.standard_normal((HIDDEN, F)) * scale / s[:, None], FMT)
    bk = bf(np.random.standard_normal(F) * 0.5)
    Wv_words, Wv_scales = pack_weight(np.random.standard_normal((HIDDEN, F)) * scale / s[:, None], FMT)
    bv = bf(np.random.standard_normal(F) * 0.5)
    return {
        "hidden_states": hidden_states,
        "Wq_words": Wq_words,
        "Wq_scales": Wq_scales,
        "bq": bq,
        "Wk_words": Wk_words,
        "Wk_scales": Wk_scales,
        "bk": bk,
        "Wv_words": Wv_words,
        "Wv_scales": Wv_scales,
        "bv": bv,
    }


def reference(hidden_states, Wq_words, Wq_scales, bq, Wk_words, Wk_scales, bk, Wv_words, Wv_scales, bv):
    Wqkv = np.concatenate([
        unpack_weight(Wq_words, Wq_scales, FMT),
        unpack_weight(Wk_words, Wk_scales, FMT),
        unpack_weight(Wv_words, Wv_scales, FMT),
    ], axis=1)
    bqkv = np.concatenate([f64(bq), f64(bk), f64(bv)], axis=0)
    qkv = (mxq(f64(hidden_states), 2, "e4m3") @ Wqkv) + bqkv
    q, k, v = np.split(qkv, 3, axis=-1)
    return (_split_heads(q), _split_heads(k), _split_heads(v))

@@ -1,0 +1,170 @@
+from contextlib import ExitStack
+
+import concourse.mybir as mybir
+from concourse.masks import make_identity
+
+F32 = mybir.dt.float32
+BF16 = mybir.dt.bfloat16
+I32 = mybir.dt.int32
+U32 = mybir.dt.uint32
+U8 = mybir.dt.uint8
+FP8X4 = mybir.dt.float8_e4m3fn_x4
+
+P = 128
+HIDDEN = 3072
+K_PASS = 512
+GROUPS = HIDDEN // K_PASS
+FEATURES = 2048
+N_TILE = 512
+BLOCKS = FEATURES // N_TILE
+HEADS_PER_BLOCK = N_TILE // 128
+
+FLOPS = 2 * P * HIDDEN * 3 * FEATURES
+
+
+def tile_attention_before_w_kernel(
+    tc,
+    hidden_states,
+    Wq_words,
+    Wq_scales,
+    bq,
+    Wk_words,
+    Wk_scales,
+    bk,
+    Wv_words,
+    Wv_scales,
+    bv,
+    out_0,
+    out_1,
+    out_2,
+):
+    nc = tc.nc
+    all_words = (Wq_words, Wk_words, Wv_words)
+    all_scales = (Wq_scales, Wk_scales, Wv_scales)
+    all_bias = (bq, bk, bv)
+    all_out = (out_0, out_1, out_2)
+
+    with ExitStack() as ctx:
+        keep = ctx.enter_context(tc.tile_pool(name="keep", bufs=1))
+        banks = ctx.enter_context(tc.psum_pool(name="banks", bufs=8))
+        ctx.enter_context(tc.manual_schedule())
+
+        x_sb = keep.tile([P, HIDDEN], BF16, name="x_sb", align_bytes=64)
+        ident_f = keep.tile([P, P], F32, name="ident_f")
+        ident_b = keep.tile([P, P], BF16, name="ident_b")
+        bias_rows = keep.tile([P, N_TILE], BF16, name="bias_rows")
+        x_codes = keep.tile([P, GROUPS * P], U32, name="x_codes", align_bytes=64)
+        x_scales = keep.tile([P, GROUPS * P], U8, name="x_scales", align_bytes=64)
+        grouped = [
+            keep.tile([P, 2 * K_PASS], BF16, name="grouped%d" % b, align_bytes=64) for b in range(3)
+        ]
+        w_sb = [
+            [keep.tile([P, FEATURES], U32, name="w%d_%d" % (w, g), align_bytes=64) for g in range(GROUPS)]
+            for w in range(3)
+        ]
+        planes = [
+            [keep.tile([P, FEATURES], U8, name="pl%d_%d" % (w, s), align_bytes=64) for s in range(2)]
+            for w in range(3)
+        ]
+        res = [
+            [keep.tile([P, N_TILE], F32, name="res%d_%d" % (w, j)) for j in range(BLOCKS)] for w in range(3)
+        ]
+
+        nc.vector.memset(bias_rows[:].bitcast(I32), 0)
+        for w in range(3):
+            for s in range(2):
+                nc.vector.memset(planes[w][s][:].bitcast(I32), 0)
+
+        make_identity(nc, ident_f[:])
+        make_identity(nc, ident_b[:])
+
+        nc.sync.dma_start(out=x_sb[:], in_=hidden_states.flatten_outer_dims())
+        for w in range(3):
+            for g in range(GROUPS):
+                nc.sync.dma_start(
+                    out=w_sb[w][g][:].bitcast(I32),
+                    in_=all_words[w][g].rearrange("p n t -> p (n t)").bitcast(I32),
+                )
+
+        for w in range(3):
+            nc.scalar.dma_start(
+                out=bias_rows[BLOCKS * w : BLOCKS * (w + 1), :],
+                in_=all_bias[w].rearrange("(r c) -> r c", c=N_TILE),
+            )
+
+        for w in range(3):
+            for s, (g0, n_g) in enumerate(((0, 4), (4, 2))):
+                for quad in range(4):
+                    nc.gpsimd.dma_start(
+                        out=planes[w][s][32 * quad : 32 * quad + 4 * n_g, :].bitcast(F32),
+                        in_=all_scales[w][g0 : g0 + n_g, 4 * quad : 4 * quad + 4, :].bitcast(F32),
+                    )
+
+        x_words = x_sb[:].bitcast(F32)
+        xt = []
+        for b in range(3):
+            xt_b = banks.tile([P, N_TILE], F32, name="xt%d" % b, tag="bank")
+            xt.append(xt_b)
+            for gg in range(2):
+                g = 2 * b + gg
+                for u in range(2):
+                    c = (2 * gg + u) * P
+                    nc.tensor.transpose(
+                        xt_b[:, c : c + P],
+                        x_words[:, 256 * g + u : 256 * (g + 1) : 2],
+                        ident_f[:],
+                    )
+        for b in (0, 2, 1):
+            dst = grouped[b][:].bitcast(F32).rearrange("p (gg s u) -> p gg s u", gg=2, u=2)
+            src = xt[b][:].rearrange("p (gg u s) -> p gg s u", gg=2, u=2)
+            if b == 1:
+                nc.scalar.copy(out=dst, in_=src)
+            else:
+                nc.vector.tensor_copy(out=dst, in_=src)
+        for b in range(3):
+            nc.vector.quantize_mx(
+                out=x_codes[:, 2 * P * b : 2 * P * (b + 1)].bitcast(FP8X4),
+                scales=x_scales[:, 2 * P * b : 2 * P * (b + 1)],
+                in_=grouped[b][:],
+            )
+
+        for w in range(3):
+            for j in range(BLOCKS):
+                r = BLOCKS * w + j
+                bp = banks.tile([P, N_TILE], F32, name="bp%d" % r, tag="bank")
+                nc.tensor.matmul(
+                    out=bp[:],
+                    lhsT=ident_b[:, r : r + 1].to_broadcast([P, P]),
+                    rhs=bias_rows[:],
+                    start=True,
+                    stop=True,
+                )
+                nc.scalar.copy(out=res[w][j][:], in_=bp[:])
+
+        for w in range(3):
+            acc = [banks.tile([P, N_TILE], F32, name="acc%d_%d" % (w, j), tag="bank") for j in range(BLOCKS)]
+            for g in range(GROUPS):
+                plane = planes[w][g // 4]
+                off = 4 * (g % 4)
+                for j in range(BLOCKS):
+                    cols = slice(N_TILE * j, N_TILE * (j + 1))
+                    nc.tensor.matmul_mx(
+                        out=acc[j][:],
+                        lhsT=x_codes[:, P * g : P * (g + 1)].bitcast(FP8X4),
+                        lhsT_scale=x_scales[:, P * g : P * (g + 1)],
+                        rhs=w_sb[w][g][:, cols].bitcast(FP8X4),
+                        rhs_scale=plane[off:P, cols],
+                        start=(g == 0),
+                        stop=(g == GROUPS - 1),
+                    )
+            for j in range(BLOCKS):
+                nc.vector.tensor_tensor(
+                    out=res[w][j][:], in0=acc[j][:], in1=res[w][j][:], op=mybir.AluOpType.add
+                )
+
+        for w in range(3):
+            for j in range(BLOCKS):
+                nc.sync.dma_start(
+                    out=all_out[w][0, HEADS_PER_BLOCK * j : HEADS_PER_BLOCK * (j + 1)].rearrange("h s d -> s h d"),
+                    in_=res[w][j][:].rearrange("s (h d) -> s h d", h=HEADS_PER_BLOCK),
+                )

@@ -15,9 +15,12 @@ HIDDEN = 3072
 K_PASS = 512
 GROUPS = HIDDEN // K_PASS
 FEATURES = 2048
-N_TILE = 512
-BLOCKS = FEATURES // N_TILE
-HEADS_PER_BLOCK = N_TILE // 128
+HEADS = FEATURES // P
+BANK = 512
+HB = 4
+BANKS_PER_W = HEADS // HB
+TOK = 4
+TOK_GROUPS = P // TOK
 
 FLOPS = 2 * P * HIDDEN * 3 * FEATURES
 
@@ -46,13 +49,15 @@ def tile_attention_before_w_kernel(
 
     with ExitStack() as ctx:
         keep = ctx.enter_context(tc.tile_pool(name="keep", bufs=1))
+        work = ctx.enter_context(tc.tile_pool(name="work", bufs=4))
         banks = ctx.enter_context(tc.psum_pool(name="banks", bufs=8))
         ctx.enter_context(tc.manual_schedule())
 
         x_sb = keep.tile([P, HIDDEN], BF16, name="x_sb", align_bytes=64)
         ident_f = keep.tile([P, P], F32, name="ident_f")
         ident_b = keep.tile([P, P], BF16, name="ident_b")
-        bias_rows = keep.tile([P, N_TILE], BF16, name="bias_rows")
+        bias_in = keep.tile([P, P], BF16, name="bias_in")
+        bias_t = keep.tile([P, P], F32, name="bias_t")
         x_codes = keep.tile([P, GROUPS * P], U32, name="x_codes", align_bytes=64)
         x_scales = keep.tile([P, GROUPS * P], U8, name="x_scales", align_bytes=64)
         grouped = [
@@ -66,11 +71,11 @@ def tile_attention_before_w_kernel(
             [keep.tile([P, FEATURES], U8, name="pl%d_%d" % (w, s), align_bytes=64) for s in range(2)]
             for w in range(3)
         ]
-        res = [
-            [keep.tile([P, N_TILE], F32, name="res%d_%d" % (w, j)) for j in range(BLOCKS)] for w in range(3)
+        z_sb = [
+            [keep.tile([P, BANK], F32, name="z%d_%d" % (w, hb)) for hb in range(BANKS_PER_W)] for w in range(3)
         ]
 
-        nc.vector.memset(bias_rows[:].bitcast(I32), 0)
+        nc.vector.memset(bias_in[:].bitcast(I32), 0)
         for w in range(3):
             for s in range(2):
                 nc.vector.memset(planes[w][s][:].bitcast(I32), 0)
@@ -88,8 +93,8 @@ def tile_attention_before_w_kernel(
 
         for w in range(3):
             nc.scalar.dma_start(
-                out=bias_rows[BLOCKS * w : BLOCKS * (w + 1), :],
-                in_=all_bias[w].rearrange("(r c) -> r c", c=N_TILE),
+                out=bias_in[HEADS * w : HEADS * (w + 1), :],
+                in_=all_bias[w].rearrange("(h d) -> h d", d=P),
             )
 
         for w in range(3):
@@ -103,7 +108,7 @@ def tile_attention_before_w_kernel(
         x_words = x_sb[:].bitcast(F32)
         xt = []
         for b in range(3):
-            xt_b = banks.tile([P, N_TILE], F32, name="xt%d" % b, tag="bank")
+            xt_b = banks.tile([P, BANK], F32, name="xt%d" % b, tag="bank")
             xt.append(xt_b)
             for gg in range(2):
                 g = 2 * b + gg
@@ -114,6 +119,9 @@ def tile_attention_before_w_kernel(
                         x_words[:, 256 * g + u : 256 * (g + 1) : 2],
                         ident_f[:],
                     )
+        bt = banks.tile([P, P], BF16, name="bt", tag="bank")
+        nc.tensor.transpose(bt[:], bias_in[:], ident_b[:])
+
         for b in (0, 2, 1):
             dst = grouped[b][:].bitcast(F32).rearrange("p (gg s u) -> p gg s u", gg=2, u=2)
             src = xt[b][:].rearrange("p (gg u s) -> p gg s u", gg=2, u=2)
@@ -127,44 +135,43 @@ def tile_attention_before_w_kernel(
                 scales=x_scales[:, 2 * P * b : 2 * P * (b + 1)],
                 in_=grouped[b][:],
             )
+        nc.vector.tensor_copy(out=bias_t[:], in_=bt[:])
 
         for w in range(3):
-            for j in range(BLOCKS):
-                r = BLOCKS * w + j
-                bp = banks.tile([P, N_TILE], F32, name="bp%d" % r, tag="bank")
-                nc.tensor.matmul(
-                    out=bp[:],
-                    lhsT=ident_b[:, r : r + 1].to_broadcast([P, P]),
-                    rhs=bias_rows[:],
-                    start=True,
-                    stop=True,
-                )
-                nc.scalar.copy(out=res[w][j][:], in_=bp[:])
-
-        for w in range(3):
-            acc = [banks.tile([P, N_TILE], F32, name="acc%d_%d" % (w, j), tag="bank") for j in range(BLOCKS)]
+            acc = [banks.tile([P, BANK], F32, name="acc%d_%d" % (w, hb), tag="bank") for hb in range(BANKS_PER_W)]
             for g in range(GROUPS):
                 plane = planes[w][g // 4]
                 off = 4 * (g % 4)
-                for j in range(BLOCKS):
-                    cols = slice(N_TILE * j, N_TILE * (j + 1))
-                    nc.tensor.matmul_mx(
-                        out=acc[j][:],
-                        lhsT=x_codes[:, P * g : P * (g + 1)].bitcast(FP8X4),
-                        lhsT_scale=x_scales[:, P * g : P * (g + 1)],
-                        rhs=w_sb[w][g][:, cols].bitcast(FP8X4),
-                        rhs_scale=plane[off:P, cols],
-                        start=(g == 0),
-                        stop=(g == GROUPS - 1),
-                    )
-            for j in range(BLOCKS):
+                for hb in range(BANKS_PER_W):
+                    for hh in range(HB):
+                        h = HB * hb + hh
+                        cols = slice(P * h, P * (h + 1))
+                        nc.tensor.matmul_mx(
+                            out=acc[hb][:, P * hh : P * (hh + 1)],
+                            lhsT=w_sb[w][g][:, cols].bitcast(FP8X4),
+                            lhsT_scale=plane[off:P, cols],
+                            rhs=x_codes[:, P * g : P * (g + 1)].bitcast(FP8X4),
+                            rhs_scale=x_scales[:, P * g : P * (g + 1)],
+                            start=(g == 0 and hh == 0),
+                            stop=(g == GROUPS - 1 and hh == HB - 1),
+                        )
+            for hb in range(BANKS_PER_W):
+                y_t = work.tile([P, BANK], F32, name="y_t%d_%d" % (w, hb), tag="y_t")
+                first = HEADS * w + HB * hb
                 nc.vector.tensor_tensor(
-                    out=res[w][j][:], in0=acc[j][:], in1=res[w][j][:], op=mybir.AluOpType.add
+                    out=y_t[:].rearrange("p (i h a) -> p i h a", i=TOK, h=HB),
+                    in0=acc[hb][:].rearrange("p (h a i) -> p i h a", h=HB, i=TOK),
+                    in1=bias_t[:, first : first + HB].unsqueeze(1).unsqueeze(3).to_broadcast([P, TOK, HB, TOK_GROUPS]),
+                    op=mybir.AluOpType.add,
                 )
+                z_ps = banks.tile([P, BANK], F32, name="zp%d_%d" % (w, hb), tag="bank")
+                for i in range(TOK):
+                    nc.tensor.transpose(z_ps[:, P * i : P * (i + 1)], y_t[:, P * i : P * (i + 1)], ident_f[:])
+                nc.scalar.copy(out=z_sb[w][hb][:], in_=z_ps[:])
 
         for w in range(3):
-            for j in range(BLOCKS):
+            for hb in range(BANKS_PER_W):
                 nc.sync.dma_start(
-                    out=all_out[w][0, HEADS_PER_BLOCK * j : HEADS_PER_BLOCK * (j + 1)].rearrange("h s d -> s h d"),
-                    in_=res[w][j][:].rearrange("s (h d) -> s h d", h=HEADS_PER_BLOCK),
+                    out=all_out[w][0, HB * hb : HB * (hb + 1)].rearrange("h (a i) d -> (h a) (i d)", i=TOK),
+                    in_=z_sb[w][hb][:],
                 )

@@ -83,6 +83,13 @@ def tile_attention_before_w_kernel(
         make_identity(nc, ident_f[:])
         make_identity(nc, ident_b[:])
 
+        for w in range(3):
+            for s, (g0, n_g) in enumerate(((0, 4), (4, 2))):
+                for quad in range(4):
+                    nc.sync.dma_start(
+                        out=planes[w][s][32 * quad : 32 * quad + 4 * n_g, :].bitcast(I32),
+                        in_=all_scales[w][g0 : g0 + n_g, 4 * quad : 4 * quad + 4, :].bitcast(I32),
+                    )
         nc.sync.dma_start(out=x_sb[:], in_=hidden_states.flatten_outer_dims())
         for w in range(3):
             for g in range(GROUPS):
@@ -96,14 +103,6 @@ def tile_attention_before_w_kernel(
                 out=bias_in[HEADS * w : HEADS * (w + 1), :],
                 in_=all_bias[w].rearrange("(h d) -> h d", d=P),
             )
-
-        for w in range(3):
-            for s, (g0, n_g) in enumerate(((0, 4), (4, 2))):
-                for quad in range(4):
-                    nc.gpsimd.dma_start(
-                        out=planes[w][s][32 * quad : 32 * quad + 4 * n_g, :].bitcast(F32),
-                        in_=all_scales[w][g0 : g0 + n_g, 4 * quad : 4 * quad + 4, :].bitcast(F32),
-                    )
 
         x_words = x_sb[:].bitcast(F32)
         xt = []

@@ -83,26 +83,43 @@ def tile_attention_before_w_kernel(
         make_identity(nc, ident_f[:])
         make_identity(nc, ident_b[:])
 
-        for w in range(3):
-            for s, (g0, n_g) in enumerate(((0, 4), (4, 2))):
-                for quad in range(4):
-                    nc.sync.dma_start(
-                        out=planes[w][s][32 * quad : 32 * quad + 4 * n_g, :].bitcast(I32),
-                        in_=all_scales[w][g0 : g0 + n_g, 4 * quad : 4 * quad + 4, :].bitcast(I32),
-                    )
+        def scale_dma(queue, view, w, s, quad):
+            g0, n_g = ((0, 4), (4, 2))[s]
+            queue.dma_start(
+                out=planes[w][s][32 * quad : 32 * quad + 4 * n_g, :].bitcast(view),
+                in_=all_scales[w][g0 : g0 + n_g, 4 * quad : 4 * quad + 4, :].bitcast(view),
+            )
+
+        def word_dma(w, g):
+            nc.sync.dma_start(
+                out=w_sb[w][g][:].bitcast(I32),
+                in_=all_words[w][g].rearrange("p n t -> p (n t)").bitcast(I32),
+            )
+
         nc.sync.dma_start(out=x_sb[:], in_=hidden_states.flatten_outer_dims())
-        for w in range(3):
+        for s in range(2):
+            for quad in (0, 1):
+                scale_dma(nc.sync, I32, 0, s, quad)
+        later = [(w, s, quad) for w in (1, 2) for s in range(2) for quad in (0, 1)]
+        for g in range(GROUPS):
+            word_dma(0, g)
+            if g >= 2:
+                for w, s, quad in later[2 * (g - 2) : 2 * (g - 1)]:
+                    scale_dma(nc.sync, I32, w, s, quad)
+        for w in (1, 2):
             for g in range(GROUPS):
-                nc.sync.dma_start(
-                    out=w_sb[w][g][:].bitcast(I32),
-                    in_=all_words[w][g].rearrange("p n t -> p (n t)").bitcast(I32),
-                )
+                word_dma(w, g)
 
         for w in range(3):
             nc.scalar.dma_start(
                 out=bias_in[HEADS * w : HEADS * (w + 1), :],
                 in_=all_bias[w].rearrange("(h d) -> h d", d=P),
             )
+
+        for w in range(3):
+            for s in range(2):
+                for quad in (2, 3):
+                    scale_dma(nc.gpsimd, F32, w, s, quad)
 
         x_words = x_sb[:].bitcast(F32)
         xt = []

@@ -18,9 +18,12 @@ FEATURES = 2048
 HEADS = FEATURES // P
 BANK = 512
 HB = 4
-BANKS_PER_W = HEADS // HB
-TOK = 4
-TOK_GROUPS = P // TOK
+
+LOADS = tuple((w, 0, HEADS, g, 1) for w in range(3) for g in range(GROUPS))[:-1] + (
+    (2, 0, 8, 5, 1),
+    (2, 8, 8, 5, 1),
+)
+STORES = ((16,), (16,), (4, 4, 4, 4))
 
 FLOPS = 2 * P * HIDDEN * 3 * FEATURES
 
@@ -49,7 +52,6 @@ def tile_attention_before_w_kernel(
 
     with ExitStack() as ctx:
         keep = ctx.enter_context(tc.tile_pool(name="keep", bufs=1))
-        work = ctx.enter_context(tc.tile_pool(name="work", bufs=4))
         banks = ctx.enter_context(tc.psum_pool(name="banks", bufs=8))
         ctx.enter_context(tc.manual_schedule())
 
@@ -64,17 +66,13 @@ def tile_attention_before_w_kernel(
             keep.tile([P, 2 * K_PASS], BF16, name="grouped%d" % b, align_bytes=64) for b in range(3)
         ]
         w_sb = [
-            [keep.tile([P, FEATURES], U32, name="w%d_%d" % (w, g), align_bytes=64) for g in range(GROUPS)]
-            for w in range(3)
+            keep.tile([P, n_g * n_h * P], U32, name="w%d_%d_%d" % (w, h0, g0), align_bytes=64)
+            for w, h0, n_h, g0, n_g in LOADS
         ]
         planes = [
             [keep.tile([P, FEATURES], U8, name="pl%d_%d" % (w, s), align_bytes=64) for s in range(2)]
             for w in range(3)
         ]
-        z_sb = [
-            [keep.tile([P, BANK], F32, name="z%d_%d" % (w, hb)) for hb in range(BANKS_PER_W)] for w in range(3)
-        ]
-
         nc.vector.memset(bias_in[:].bitcast(I32), 0)
         for w in range(3):
             for s in range(2):
@@ -90,25 +88,27 @@ def tile_attention_before_w_kernel(
                 in_=all_scales[w][g0 : g0 + n_g, 4 * quad : 4 * quad + 4, :].bitcast(view),
             )
 
-        def word_dma(w, g):
+        def word_dma(n):
+            w, h0, n_h, g0, n_g = LOADS[n]
             nc.sync.dma_start(
-                out=w_sb[w][g][:].bitcast(I32),
-                in_=all_words[w][g].rearrange("p n t -> p (n t)").bitcast(I32),
+                out=w_sb[n][:].bitcast(I32).rearrange("p (g c) -> p g c", g=n_g),
+                in_=all_words[w][g0 : g0 + n_g, :, P * h0 : P * (h0 + n_h)]
+                .rearrange("g p c t -> p g (c t)")
+                .bitcast(I32),
             )
 
+        def words_of(w, g, h):
+            for n, (lw, h0, n_h, g0, n_g) in enumerate(LOADS):
+                if w == lw and h0 <= h < h0 + n_h and g0 <= g < g0 + n_g:
+                    c = ((g - g0) * n_h + h - h0) * P
+                    return w_sb[n][:, c : c + P].bitcast(FP8X4)
+
         nc.sync.dma_start(out=x_sb[:], in_=hidden_states.flatten_outer_dims())
-        for s in range(2):
-            for quad in (0, 1):
-                scale_dma(nc.sync, I32, 0, s, quad)
-        later = [(w, s, quad) for w in (1, 2) for s in range(2) for quad in (0, 1)]
-        for g in range(GROUPS):
-            word_dma(0, g)
-            if g >= 2:
-                for w, s, quad in later[2 * (g - 2) : 2 * (g - 1)]:
-                    scale_dma(nc.sync, I32, w, s, quad)
-        for w in (1, 2):
-            for g in range(GROUPS):
-                word_dma(w, g)
+        lower = [(w, s, quad) for w in range(3) for s in range(2) for quad in (0, 1)]
+        for n in range(len(LOADS)):
+            word_dma(n)
+            for w, s, quad in lower[2 * n : 2 * (n + 1)]:
+                scale_dma(nc.sync, I32, w, s, quad)
 
         for w in range(3):
             nc.scalar.dma_start(
@@ -153,41 +153,48 @@ def tile_attention_before_w_kernel(
             )
         nc.vector.tensor_copy(out=bias_t[:], in_=bt[:])
 
+        stores = []
         for w in range(3):
-            acc = [banks.tile([P, BANK], F32, name="acc%d_%d" % (w, hb), tag="bank") for hb in range(BANKS_PER_W)]
+            acc = [banks.tile([P, BANK], F32, name="acc%d_%d" % (w, n), tag="bank") for n in range(HEADS // HB)]
             for g in range(GROUPS):
                 plane = planes[w][g // 4]
                 off = 4 * (g % 4)
-                for hb in range(BANKS_PER_W):
+                for n in range(HEADS // HB):
                     for hh in range(HB):
-                        h = HB * hb + hh
-                        cols = slice(P * h, P * (h + 1))
+                        h = HB * n + hh
                         nc.tensor.matmul_mx(
-                            out=acc[hb][:, P * hh : P * (hh + 1)],
-                            lhsT=w_sb[w][g][:, cols].bitcast(FP8X4),
-                            lhsT_scale=plane[off:P, cols],
+                            out=acc[n][:, P * hh : P * (hh + 1)],
+                            lhsT=words_of(w, g, h),
+                            lhsT_scale=plane[off:P, P * h : P * (h + 1)],
                             rhs=x_codes[:, P * g : P * (g + 1)].bitcast(FP8X4),
                             rhs_scale=x_scales[:, P * g : P * (g + 1)],
                             start=(g == 0 and hh == 0),
                             stop=(g == GROUPS - 1 and hh == HB - 1),
                         )
-            for hb in range(BANKS_PER_W):
-                y_t = work.tile([P, BANK], F32, name="y_t%d_%d" % (w, hb), tag="y_t")
-                first = HEADS * w + HB * hb
-                nc.vector.tensor_tensor(
-                    out=y_t[:].rearrange("p (i h a) -> p i h a", i=TOK, h=HB),
-                    in0=acc[hb][:].rearrange("p (h a i) -> p i h a", h=HB, i=TOK),
-                    in1=bias_t[:, first : first + HB].unsqueeze(1).unsqueeze(3).to_broadcast([P, TOK, HB, TOK_GROUPS]),
-                    op=mybir.AluOpType.add,
-                )
-                z_ps = banks.tile([P, BANK], F32, name="zp%d_%d" % (w, hb), tag="bank")
-                for i in range(TOK):
-                    nc.tensor.transpose(z_ps[:, P * i : P * (i + 1)], y_t[:, P * i : P * (i + 1)], ident_f[:])
-                nc.scalar.copy(out=z_sb[w][hb][:], in_=z_ps[:])
+            h0 = 0
+            for n_h in STORES[w]:
+                tok, groups = n_h, P // n_h
+                y = keep.tile([P, n_h * P], F32, name="y%d_%d" % (w, h0))
+                z = keep.tile([P, n_h * P], F32, name="z%d_%d" % (w, h0))
+                for n in range(n_h // HB):
+                    first = HEADS * w + h0 + HB * n
+                    nc.vector.tensor_tensor(
+                        out=y[:].rearrange("p (i h a) -> p i h a", i=tok, h=n_h)[:, :, HB * n : HB * (n + 1), :],
+                        in0=acc[h0 // HB + n][:].rearrange("p (h a i) -> p i h a", h=HB, i=tok),
+                        in1=bias_t[:, first : first + HB].unsqueeze(1).unsqueeze(3).to_broadcast([P, tok, HB, groups]),
+                        op=mybir.AluOpType.add,
+                    )
+                for n in range(n_h // HB):
+                    z_ps = banks.tile([P, BANK], F32, name="zp%d_%d_%d" % (w, h0, n), tag="bank")
+                    for u in range(4):
+                        i = 4 * n + u
+                        nc.tensor.transpose(z_ps[:, P * u : P * (u + 1)], y[:, P * i : P * (i + 1)], ident_f[:])
+                    nc.scalar.copy(out=z[:, BANK * n : BANK * (n + 1)], in_=z_ps[:])
+                stores.append((w, h0, n_h, z))
+                h0 += n_h
 
-        for w in range(3):
-            for hb in range(BANKS_PER_W):
-                nc.sync.dma_start(
-                    out=all_out[w][0, HB * hb : HB * (hb + 1)].rearrange("h (a i) d -> (h a) (i d)", i=TOK),
-                    in_=z_sb[w][hb][:],
-                )
+        for w, h0, n_h, z in stores:
+            nc.sync.dma_start(
+                out=all_out[w][0, h0 : h0 + n_h].rearrange("h (a i) d -> (h a) (i d)", i=n_h),
+                in_=z[:],
+            )

from contextlib import ExitStack

import concourse.mybir as mybir
from concourse.masks import make_identity

F32 = mybir.dt.float32
BF16 = mybir.dt.bfloat16
I32 = mybir.dt.int32
U32 = mybir.dt.uint32
U8 = mybir.dt.uint8
FP8X4 = mybir.dt.float8_e4m3fn_x4

P = 128
HIDDEN = 3072
K_PASS = 512
GROUPS = HIDDEN // K_PASS
FEATURES = 2048
HEADS = FEATURES // P
BANK = 512
HB = 4

LOADS = tuple((w, 0, HEADS, g, 1) for w in range(3) for g in range(GROUPS))[:-1] + (
    (2, 0, 8, 5, 1),
    (2, 8, 8, 5, 1),
)
STORES = ((16,), (16,), (4, 4, 4, 4))

FLOPS = 2 * P * HIDDEN * 3 * FEATURES


def tile_attention_before_w_kernel(
    tc,
    hidden_states,
    Wq_words,
    Wq_scales,
    bq,
    Wk_words,
    Wk_scales,
    bk,
    Wv_words,
    Wv_scales,
    bv,
    out_0,
    out_1,
    out_2,
):
    nc = tc.nc
    all_words = (Wq_words, Wk_words, Wv_words)
    all_scales = (Wq_scales, Wk_scales, Wv_scales)
    all_bias = (bq, bk, bv)
    all_out = (out_0, out_1, out_2)

    with ExitStack() as ctx:
        keep = ctx.enter_context(tc.tile_pool(name="keep", bufs=1))
        banks = ctx.enter_context(tc.psum_pool(name="banks", bufs=8))
        ctx.enter_context(tc.manual_schedule())

        x_sb = keep.tile([P, HIDDEN], BF16, name="x_sb", align_bytes=64)
        ident_f = keep.tile([P, P], F32, name="ident_f")
        ident_b = keep.tile([P, P], BF16, name="ident_b")
        bias_in = keep.tile([P, P], BF16, name="bias_in")
        bias_t = keep.tile([P, P], F32, name="bias_t")
        x_codes = keep.tile([P, GROUPS * P], U32, name="x_codes", align_bytes=64)
        x_scales = keep.tile([P, GROUPS * P], U8, name="x_scales", align_bytes=64)
        grouped = [
            keep.tile([P, 2 * K_PASS], BF16, name="grouped%d" % b, align_bytes=64) for b in range(3)
        ]
        w_sb = [
            keep.tile([P, n_g * n_h * P], U32, name="w%d_%d_%d" % (w, h0, g0), align_bytes=64)
            for w, h0, n_h, g0, n_g in LOADS
        ]
        planes = [
            [keep.tile([P, FEATURES], U8, name="pl%d_%d" % (w, s), align_bytes=64) for s in range(2)]
            for w in range(3)
        ]
        nc.vector.memset(bias_in[:].bitcast(I32), 0)
        for w in range(3):
            for s in range(2):
                nc.vector.memset(planes[w][s][:].bitcast(I32), 0)

        make_identity(nc, ident_f[:])
        make_identity(nc, ident_b[:])

        def scale_dma(queue, view, w, s, quad):
            g0, n_g = ((0, 4), (4, 2))[s]
            queue.dma_start(
                out=planes[w][s][32 * quad : 32 * quad + 4 * n_g, :].bitcast(view),
                in_=all_scales[w][g0 : g0 + n_g, 4 * quad : 4 * quad + 4, :].bitcast(view),
            )

        def word_dma(n):
            w, h0, n_h, g0, n_g = LOADS[n]
            nc.sync.dma_start(
                out=w_sb[n][:].bitcast(I32).rearrange("p (g c) -> p g c", g=n_g),
                in_=all_words[w][g0 : g0 + n_g, :, P * h0 : P * (h0 + n_h)]
                .rearrange("g p c t -> p g (c t)")
                .bitcast(I32),
            )

        def words_of(w, g, h):
            for n, (lw, h0, n_h, g0, n_g) in enumerate(LOADS):
                if w == lw and h0 <= h < h0 + n_h and g0 <= g < g0 + n_g:
                    c = ((g - g0) * n_h + h - h0) * P
                    return w_sb[n][:, c : c + P].bitcast(FP8X4)

        nc.sync.dma_start(out=x_sb[:], in_=hidden_states.flatten_outer_dims())
        lower = [(w, s, quad) for w in range(3) for s in range(2) for quad in (0, 1)]
        for n in range(len(LOADS)):
            word_dma(n)
            for w, s, quad in lower[2 * n : 2 * (n + 1)]:
                scale_dma(nc.sync, I32, w, s, quad)

        for w in range(3):
            nc.scalar.dma_start(
                out=bias_in[HEADS * w : HEADS * (w + 1), :],
                in_=all_bias[w].rearrange("(h d) -> h d", d=P),
            )

        for w in range(3):
            for s in range(2):
                for quad in (2, 3):
                    scale_dma(nc.gpsimd, F32, w, s, quad)

        x_words = x_sb[:].bitcast(F32)
        xt = []
        for b in range(3):
            xt_b = banks.tile([P, BANK], F32, name="xt%d" % b, tag="bank")
            xt.append(xt_b)
            for gg in range(2):
                g = 2 * b + gg
                for u in range(2):
                    c = (2 * gg + u) * P
                    nc.tensor.transpose(
                        xt_b[:, c : c + P],
                        x_words[:, 256 * g + u : 256 * (g + 1) : 2],
                        ident_f[:],
                    )
        bt = banks.tile([P, P], BF16, name="bt", tag="bank")
        nc.tensor.transpose(bt[:], bias_in[:], ident_b[:])

        for b in (0, 2, 1):
            dst = grouped[b][:].bitcast(F32).rearrange("p (gg s u) -> p gg s u", gg=2, u=2)
            src = xt[b][:].rearrange("p (gg u s) -> p gg s u", gg=2, u=2)
            if b == 1:
                nc.scalar.copy(out=dst, in_=src)
            else:
                nc.vector.tensor_copy(out=dst, in_=src)
        for b in range(3):
            nc.vector.quantize_mx(
                out=x_codes[:, 2 * P * b : 2 * P * (b + 1)].bitcast(FP8X4),
                scales=x_scales[:, 2 * P * b : 2 * P * (b + 1)],
                in_=grouped[b][:],
            )
        nc.vector.tensor_copy(out=bias_t[:], in_=bt[:])

        stores = []
        for w in range(3):
            acc = [banks.tile([P, BANK], F32, name="acc%d_%d" % (w, n), tag="bank") for n in range(HEADS // HB)]
            for g in range(GROUPS):
                plane = planes[w][g // 4]
                off = 4 * (g % 4)
                for n in range(HEADS // HB):
                    for hh in range(HB):
                        h = HB * n + hh
                        nc.tensor.matmul_mx(
                            out=acc[n][:, P * hh : P * (hh + 1)],
                            lhsT=words_of(w, g, h),
                            lhsT_scale=plane[off:P, P * h : P * (h + 1)],
                            rhs=x_codes[:, P * g : P * (g + 1)].bitcast(FP8X4),
                            rhs_scale=x_scales[:, P * g : P * (g + 1)],
                            start=(g == 0 and hh == 0),
                            stop=(g == GROUPS - 1 and hh == HB - 1),
                        )
            h0 = 0
            for n_h in STORES[w]:
                tok, groups = n_h, P // n_h
                y = keep.tile([P, n_h * P], F32, name="y%d_%d" % (w, h0))
                z = keep.tile([P, n_h * P], F32, name="z%d_%d" % (w, h0))
                for n in range(n_h // HB):
                    first = HEADS * w + h0 + HB * n
                    nc.vector.tensor_tensor(
                        out=y[:].rearrange("p (i h a) -> p i h a", i=tok, h=n_h)[:, :, HB * n : HB * (n + 1), :],
                        in0=acc[h0 // HB + n][:].rearrange("p (h a i) -> p i h a", h=HB, i=tok),
                        in1=bias_t[:, first : first + HB].unsqueeze(1).unsqueeze(3).to_broadcast([P, tok, HB, groups]),
                        op=mybir.AluOpType.add,
                    )
                for n in range(n_h // HB):
                    z_ps = banks.tile([P, BANK], F32, name="zp%d_%d_%d" % (w, h0, n), tag="bank")
                    for u in range(4):
                        i = 4 * n + u
                        nc.tensor.transpose(z_ps[:, P * u : P * (u + 1)], y[:, P * i : P * (i + 1)], ident_f[:])
                    nc.scalar.copy(out=z[:, BANK * n : BANK * (n + 1)], in_=z_ps[:])
                stores.append((w, h0, n_h, z))
                h0 += n_h

        for w, h0, n_h, z in stores:
            nc.sync.dma_start(
                out=all_out[w][0, h0 : h0 + n_h].rearrange("h (a i) d -> (h a) (i d)", i=n_h),
                in_=z[:],
            )
